import numpy as np
import ml_dtypes


def mxq(x, axis, fmt="e4m3"):
    dtype, down = {"e4m3": (ml_dtypes.float8_e4m3fn, 7), "e5m2": (ml_dtypes.float8_e5m2, 14)}[fmt]
    v = np.moveaxis(np.asarray(x, np.float32).astype(ml_dtypes.bfloat16).astype(np.float64), axis, -1)
    blocks = v.reshape(v.shape[:-1] + (-1, 32))
    amax = np.abs(blocks).max(-1, keepdims=True)
    byte = np.maximum(np.where(amax > 0, np.frexp(amax)[1] - 1 + 127, 0) - down, 1)
    scale = np.exp2(byte - 127.0)
    codes = (blocks / scale).astype(np.float32).astype(dtype).astype(np.float64)
    return np.moveaxis((codes * scale).reshape(v.shape), -1, axis)


WIDE = False


def mx_kscale(k):
    if not WIDE:
        return np.ones(k)
    levels = np.array([10, -10, 5, -5, 0])
    a = np.random.permutation(np.resize(levels, k // 512 * 4)).reshape(k // 512, 4)
    idx = np.arange(k)
    return np.exp2(a[idx // 512, idx % 128 // 32])


BF16 = ml_dtypes.bfloat16


def bf(x):
    return np.asarray(x, np.float32).astype(BF16)


def f64(x):
    return np.asarray(x).astype(np.float64)


E2M1 = np.array([0.0, 0.5, 1.0, 1.5, 2.0, 3.0, 4.0, 6.0, -0.0, -0.5, -1.0, -1.5, -2.0, -3.0, -4.0, -6.0])


def pack_weight(w, fmt):
    k, n = w.shape
    w = f64(bf(w)).reshape(k // 32, 32, n)
    amax = np.abs(w).max(1)
    if fmt == "e4m3":
        byte = np.frexp(amax)[1] - 1 + 127 - 7
    else:
        mant, ex = np.frexp(amax / 6.0)
        byte = np.where(mant > 0.5, ex, ex - 1) + 127
    byte = np.clip(np.where(amax > 0, byte, 1), 1, 254)
    scaled = (w * np.exp2(127.0 - byte)[:, None, :]).reshape(k, n).astype(np.float32)
    by_word = np.ascontiguousarray(scaled.reshape(k // 512, 128, 4, n).transpose(0, 1, 3, 2))
    if fmt == "e4m3":
        words = by_word.astype(ml_dtypes.float8_e4m3fn).view(np.uint8)
    else:
        c = by_word.astype(ml_dtypes.float4_e2m1fn).view(np.uint8) & 0xF
        words = c[..., 0::2] | (c[..., 1::2] << 4)
    return np.ascontiguousarray(words), np.ascontiguousarray(byte.astype(np.uint8).reshape(k // 512, 16, n))


def unpack_weight(words, scales, fmt):
    g, p, n, _ = words.shape
    if fmt == "e4m3":
        vals = np.ascontiguousarray(words).view(ml_dtypes.float8_e4m3fn).astype(np.float64)
    else:
        nib = np.empty((g, p, n, 4), np.uint8)
        nib[..., 0::2] = words & 0xF
        nib[..., 1::2] = words >> 4
        vals = E2M1[nib]
    vals = vals * np.repeat(np.exp2(scales.astype(np.float64) - 127.0), 8, axis=1)[..., None]
    return vals.transpose(0, 1, 3, 2).reshape(g * 512, n)


B, D, U1, U2 = 128, 2048, 4096, 2048
THRESHOLD = 1.0


def setup_inputs():
    s, t = mx_kscale(D), mx_kscale(U1)
    c = s / s.mean()
    u = np.random.random(B)
    target = np.where(np.random.random(B) < 0.5, 0.5 + 0.35 * u, 1.15 + 0.45 * u)
    g = np.random.standard_normal((B, D)) * c
    x = g * (target / np.mean(np.abs(g), axis=1))[:, None]
    w1 = np.random.standard_normal((U1, D)) / np.sqrt(D) / c[None, :] * t[:, None]
    b1 = bf(np.random.standard_normal(U1) * 0.3 * t)
    w2 = np.random.standard_normal((U2, D)) / np.sqrt(D) / c[None, :] * t[:U2, None]
    b2 = bf(np.random.standard_normal(U2) * 0.3 * t[:U2])
    wf = np.random.standard_normal((D, U1)) * 1.5 / np.sqrt(U1) / t[None, :]
    bias_f = bf(np.random.standard_normal(D) * 0.3)
    W1_words, W1_scales = pack_weight(w1.T, "e4m3")
    W2_words, W2_scales = pack_weight(w2.T, "e4m3")
    Wf_words, Wf_scales = pack_weight(wf.T, "e4m3")
    return {"x": bf(x),
            "W1_words": W1_words,
            "W1_scales": W1_scales,
            "b1": b1,
            "W2_words": W2_words,
            "W2_scales": W2_scales,
            "b2": b2,
            "Wf_words": Wf_words,
            "Wf_scales": Wf_scales,
            "bf": bias_f}


def reference(x, W1_words, W1_scales, b1, W2_words, W2_scales, b2, Wf_words, Wf_scales, bf):
    x = f64(x)
    mask = np.mean(np.abs(x), axis=1) > THRESHOLD
    xq = mxq(x, 1, "e4m3")
    o1 = np.maximum((xq @ unpack_weight(W1_words, W1_scales, "e4m3")) + f64(b1), 0.0)
    o2 = np.maximum((xq @ unpack_weight(W2_words, W2_scales, "e4m3")) + f64(b2), 0.0)
    final_dim = W1_words.shape[2]
    o2p = np.pad(o2, ((0, 0), (0, final_dim - o2.shape[1])))
    branch_out = np.where(mask[:, None], o1, o2p)
    return (mxq(branch_out, 1, "e4m3") @ unpack_weight(Wf_words, Wf_scales, "e4m3")) + f64(bf)

@@ -1,0 +1,285 @@
+from contextlib import ExitStack
+
+import concourse.mybir as mybir
+from concourse.masks import make_identity
+
+FP8X4 = mybir.dt.float8_e4m3fn_x4
+F32 = mybir.dt.float32
+BF16 = mybir.dt.bfloat16
+I32 = mybir.dt.int32
+U32 = mybir.dt.uint32
+U8 = mybir.dt.uint8
+ALU = mybir.AluOpType
+ACT = mybir.ActivationFunctionType
+
+P = 128
+D_IN = 2048
+U1 = 4096
+U2 = 2048
+D_OUT = 2048
+NT = 512
+THRESHOLD = 1.0
+W_BUFS = 14
+
+FLOPS = 2 * P * (D_IN * U1 + D_IN * U2 + U1 * D_OUT)
+
+
+def tile_dynamiclayer_w_kernel(
+    tc, x, W1_words, W1_scales, b1, W2_words, W2_scales, b2, Wf_words, Wf_scales, bf, out
+):
+    nc = tc.nc
+    with ExitStack() as ctx:
+        keep = ctx.enter_context(tc.tile_pool(name="keep", bufs=1))
+        wpool = ctx.enter_context(tc.tile_pool(name="wpool", bufs=W_BUFS))
+        lpool = ctx.enter_context(tc.tile_pool(name="lpool", bufs=4))
+        psum = ctx.enter_context(tc.psum_pool(name="psum", bufs=1))
+        ctx.enter_context(tc.manual_schedule())
+
+        def bank(i, shape, dtype, name):
+            return psum.tile(shape, dtype, tag="bank%d" % i, name=name)
+
+        warm = keep.tile([P, 1], F32, name="warm")
+        warm2 = keep.tile([P, 1], F32, name="warm2")
+        pl1 = keep.tile([P, U1], U8, name="pl1", align_bytes=64)
+        pl2 = keep.tile([P, U2], U8, name="pl2", align_bytes=64)
+        plf = keep.tile([P, 2, D_OUT], U8, name="plf", align_bytes=64)
+        sel = keep.tile([P, P], F32, name="sel")
+        nc.vector.memset(warm[:], 0.0)
+        nc.vector.memset(pl1[:].bitcast(I32), 0)
+        nc.vector.memset(pl2[:].bitcast(I32), 0)
+        nc.vector.memset(plf[:].bitcast(I32), 0)
+        nc.vector.memset(sel[:], 0.0)
+        nc.vector.memset(sel[:, 2:3], 1.0)
+        nc.scalar.activation(out=warm2[:], in_=warm[:], func=ACT.Abs)
+
+        ident_f = keep.tile([P, P], F32, name="ident_f")
+        ident_b = keep.tile([P, P], BF16, name="ident_b")
+        brow = keep.tile([P, U1 + D_OUT], BF16, name="brow")
+        make_identity(nc, ident_f[:])
+        nc.gpsimd.memset(brow[:].bitcast(F32), 0.0)
+        make_identity(nc, ident_b[:])
+
+        x_sb = keep.tile([P, D_IN], BF16, name="x_sb")
+        nc.sync.dma_start(out=x_sb[:], in_=x)
+        for q in (0, 2, 1, 3):
+            nc.sync.dma_start(
+                out=pl1[32 * q : 32 * q + 16, :].bitcast(I32),
+                in_=W1_scales[:, 4 * q : 4 * q + 4, :].bitcast(I32),
+            )
+        for q in (0, 2, 1, 3):
+            nc.sync.dma_start(
+                out=pl2[32 * q : 32 * q + 16, :].bitcast(I32),
+                in_=W2_scales[:, 4 * q : 4 * q + 4, :].bitcast(I32),
+            )
+        for a in range(2):
+            for q in (0, 2, 1, 3):
+                nc.sync.dma_start(
+                    out=plf[32 * q : 32 * q + 16, a, :].bitcast(I32),
+                    in_=Wf_scales[4 * a : 4 * a + 4, 4 * q : 4 * q + 4, :].bitcast(I32),
+                )
+
+        chunks = []
+        for kg in range(4):
+            chunks.append(("a1", kg))
+            chunks.append(("a2", kg))
+        for kg in range(4):
+            chunks.append(("b1", kg))
+        for g in range(6):
+            chunks.append(("f", g))
+        n_chunks = len(chunks)
+        w_tiles = {}
+        last_tiles = []
+
+        def load_chunk(i):
+            kind, g = chunks[i]
+            w = wpool.tile([P, 4 * NT], U32, tag="w", name="w_%s_%d" % (kind, g), align_bytes=64)
+            if kind == "a1":
+                src = W1_words[g].rearrange("p n t -> p (n t)")[:, 0 : 4 * U2]
+            elif kind == "b1":
+                src = W1_words[g].rearrange("p n t -> p (n t)")[:, 4 * U2 : 4 * U1]
+            elif kind == "a2":
+                src = W2_words[g].rearrange("p n t -> p (n t)")
+            else:
+                src = Wf_words[g].rearrange("p n t -> p (n t)")
+            nc.sync.dma_start(out=w[:].bitcast(I32), in_=src.bitcast(I32))
+            w_tiles[i] = w
+            if i == n_chunks - 1:
+                tail_src = Wf_words[6:8].rearrange("g p n t -> p g (n t)")
+                for j in range(4):
+                    wl = lpool.tile([P, 2, NT], U32, tag="wl", name="wl_%d" % j, align_bytes=64)
+                    nc.sync.dma_start(
+                        out=wl[:].bitcast(I32),
+                        in_=tail_src[:, :, 4 * NT * j : 4 * NT * (j + 1)].bitcast(I32),
+                    )
+                    last_tiles.append(wl)
+
+        for i in range(W_BUFS):
+            load_chunk(i)
+
+        xw = keep.tile([P, 4, 2, P], F32, name="xw")
+        nc.vector.tensor_copy(
+            out=xw[:], in_=x_sb[:].bitcast(F32).rearrange("b (g p u) -> b g u p", g=4, u=2)
+        )
+        junk = keep.tile([P, D_IN], BF16, name="junk")
+        ssum = keep.tile([P, 1], F32, name="ssum")
+        nc.scalar.activation(out=junk[:], in_=x_sb[:], func=ACT.Abs, accum_out=ssum[:])
+        nc.scalar.dma_start(out=brow[0:1, 0:U1], in_=b1.rearrange("(o n) -> o n", o=1))
+        nc.scalar.dma_start(out=brow[1:2, 0:U2], in_=b2.rearrange("(o n) -> o n", o=1))
+        nc.scalar.dma_start(out=brow[2:3, U1 : U1 + D_OUT], in_=bf.rearrange("(o n) -> o n", o=1))
+        nc.vector.tensor_single_scalar(
+            out=sel[:, 0:1], in_=ssum[:], scalar=THRESHOLD * D_IN, op=ALU.is_gt
+        )
+        nc.vector.tensor_single_scalar(
+            out=sel[:, 1:2], in_=ssum[:], scalar=THRESHOLD * D_IN, op=ALU.is_le
+        )
+        routes = []
+        for a in range(2):
+            ia = keep.tile([P, P], F32, name="route_%d" % a)
+            nc.vector.tensor_scalar(
+                out=ia[:], in0=ident_f[:], scalar1=sel[:, a : a + 1], scalar2=None, op0=ALU.mult
+            )
+            routes.append(ia)
+
+        selT_ps = bank(4, [P, P], F32, "selT_ps")
+        nc.tensor.transpose(selT_ps[:], sel[:], ident_f[:])
+        selT = keep.tile([P, P], BF16, name="selT")
+        xt = {}
+        for a in range(2):
+            for gp in range(2):
+                t_ps = bank(2 * a + gp, [P, 4, P], F32, "xt_%d_%d" % (a, gp))
+                for gi in range(2):
+                    for u in range(2):
+                        nc.tensor.transpose(
+                            t_ps[:, 2 * gi + u, :], xw[:, 2 * gp + gi, u, :], routes[a][:]
+                        )
+                xt[(a, gp)] = t_ps
+        nc.vector.tensor_copy(out=selT[:], in_=selT_ps[:])
+        gx = []
+        xc = []
+        xs = []
+        for a in range(2):
+            gx.append(keep.tile([P, D_IN], BF16, name="gx_%d" % a, align_bytes=64))
+            xc.append(keep.tile([P, D_IN // 4], U32, name="xc_%d" % a, align_bytes=64))
+            xs.append(keep.tile([P, D_IN // 4], U8, name="xs_%d" % a, align_bytes=64))
+        for a in range(2):
+            view = gx[a][:].bitcast(F32).rearrange("p (g r u) -> p g r u", g=4, u=2)
+            nc.vector.tensor_copy(
+                out=view[:, 0:2, :, :], in_=xt[(a, 0)][:].rearrange("p (g u) r -> p g r u", u=2)
+            )
+            nc.scalar.copy(
+                out=view[:, 2:4, :, :], in_=xt[(a, 1)][:].rearrange("p (g u) r -> p g r u", u=2)
+            )
+        for a in range(2):
+            nc.vector.quantize_mx(out=xc[a][:].bitcast(FP8X4), scales=xs[a][:], in_=gx[a][:])
+
+        bsel = keep.tile([P, 8, 4, P], BF16, name="bsel")
+        bfb = keep.tile([P, D_OUT], BF16, name="bfb")
+
+        def bias_round(rnd):
+            for c in range(4 * rnd, 4 * rnd + 4):
+                pb = bank(4 + c % 4, [P, NT], F32, "pb_%d" % c)
+                nc.tensor.matmul(
+                    pb[:], lhsT=selT[:], rhs=brow[:, NT * c : NT * (c + 1)], start=True, stop=True
+                )
+                if c < 8:
+                    nc.scalar.copy(
+                        out=bsel[:, c, :, :], in_=pb[:].rearrange("b (p t) -> b t p", t=4)
+                    )
+                else:
+                    nc.scalar.copy(out=bfb[:, NT * (c - 8) : NT * (c - 7)], in_=pb[:])
+
+        hs = keep.tile([P, 8, 4, P], BF16, name="hs")
+        hg = keep.tile([P, 8, P, 4], BF16, name="hg", align_bytes=64)
+        hc = keep.tile([P, 8 * P], U32, name="hc", align_bytes=64)
+        hsc = keep.tile([P, 8 * P], U8, name="hsc", align_bytes=64)
+        acc = {}
+
+        def first_layer_passes(i):
+            kind, kg = chunks[i]
+            a = 1 if kind == "a2" else 0
+            base = 4 if kind == "b1" else 0
+            plane = pl2 if kind == "a2" else pl1
+            for j in range(4):
+                if (kind == "a1" or kind == "b1") and kg == 0:
+                    acc[base + j] = bank(base + j, [P, NT], F32, "acc_%d" % (base + j))
+                col = NT * (base + j)
+                nc.tensor.matmul_mx(
+                    out=acc[base + j][:],
+                    lhsT=xc[a][:, P * kg : P * (kg + 1)].bitcast(FP8X4),
+                    lhsT_scale=xs[a][:, P * kg : P * (kg + 1)],
+                    rhs=w_tiles[i][:, NT * j : NT * (j + 1)].bitcast(FP8X4),
+                    rhs_scale=plane[4 * kg : P, col : col + NT],
+                    start=((kind == "a1" or kind == "b1") and kg == 0),
+                    stop=((kind == "a2" or kind == "b1") and kg == 3),
+                )
+
+        def evacuate(half):
+            for g in range(4 * half, 4 * half + 4):
+                nc.vector.tensor_tensor(
+                    out=hs[:, g, :, :],
+                    in0=acc[g][:].rearrange("b (p t) -> b t p", t=4),
+                    in1=bsel[:, g, :, :],
+                    op=ALU.add,
+                )
+
+        def requantise(half):
+            hts = []
+            for g in range(4 * half, 4 * half + 4):
+                ht = bank(g, [P, 4, P], BF16, "ht_%d" % g)
+                for t in range(4):
+                    nc.tensor.transpose(ht[:, t, :], hs[:, g, t, :], ident_b[:])
+                hts.append(ht)
+            for g in range(4 * half, 4 * half + 4):
+                src = hts[g - 4 * half][:].rearrange("p t r -> p r t")
+                if g % 2 == 0:
+                    nc.scalar.activation(out=hg[:, g, :, :], in_=src, func=ACT.Relu)
+                else:
+                    nc.vector.tensor_scalar_max(out=hg[:, g, :, :], in0=src, scalar1=0.0)
+            nc.vector.quantize_mx(
+                out=hc[:, 4 * P * half : 4 * P * (half + 1)].bitcast(FP8X4),
+                scales=hsc[:, 4 * P * half : 4 * P * (half + 1)],
+                in_=hg[:, 4 * half : 4 * half + 4, :, :].rearrange("p g r t -> p (g r t)"),
+            )
+
+        oacc = {}
+
+        def out_pass(g, j, rhs):
+            if g == 0:
+                oacc[j] = bank(j, [P, NT], F32, "oacc_%d" % j)
+            nc.tensor.matmul_mx(
+                out=oacc[j][:],
+                lhsT=hc[:, P * g : P * (g + 1)].bitcast(FP8X4),
+                lhsT_scale=hsc[:, P * g : P * (g + 1)],
+                rhs=rhs.bitcast(FP8X4),
+                rhs_scale=plf[4 * (g % 4) : P, g // 4, NT * j : NT * (j + 1)],
+                start=(g == 0),
+                stop=(g == 7),
+            )
+
+        for i in range(n_chunks):
+            kind, g = chunks[i]
+            if i < 3:
+                bias_round(i)
+            if kind == "f":
+                for j in range(4):
+                    out_pass(g, j, w_tiles[i][:, NT * j : NT * (j + 1)])
+            else:
+                first_layer_passes(i)
+            if i + W_BUFS < n_chunks:
+                load_chunk(i + W_BUFS)
+            if i == 7:
+                evacuate(0)
+            if i == 8:
+                requantise(0)
+            if i == 11:
+                evacuate(1)
+            if i == 12:
+                requantise(1)
+
+        osb = keep.tile([P, D_OUT], F32, name="osb")
+        for j in range(4):
+            out_pass(6, j, last_tiles[j][:, 0, :])
+            out_pass(7, j, last_tiles[j][:, 1, :])
+            cols = slice(NT * j, NT * (j + 1))
+            nc.vector.tensor_tensor(out=osb[:, cols], in0=oacc[j][:], in1=bfb[:, cols], op=ALU.add)
+            nc.sync.dma_start(out=out[:, cols], in_=osb[:, cols])

@@ -20,6 +20,8 @@ D_OUT = 2048
 NT = 512
 THRESHOLD = 1.0
 W_BUFS = 14
+BLOCKS = ((0, 512), (512, 512), (1024, 512), (1536, 256), (1792, 128), (1920, 128))
+BLOCK_BANK = (0, 1, 2, 3, 5, 6)
 
 FLOPS = 2 * P * (D_IN * U1 + D_IN * U2 + U1 * D_OUT)
 
@@ -31,7 +33,7 @@ def tile_dynamiclayer_w_kernel(
     with ExitStack() as ctx:
         keep = ctx.enter_context(tc.tile_pool(name="keep", bufs=1))
         wpool = ctx.enter_context(tc.tile_pool(name="wpool", bufs=W_BUFS))
-        lpool = ctx.enter_context(tc.tile_pool(name="lpool", bufs=4))
+        lpool = ctx.enter_context(tc.tile_pool(name="lpool", bufs=1))
         psum = ctx.enter_context(tc.psum_pool(name="psum", bufs=1))
         ctx.enter_context(tc.manual_schedule())
 
@@ -105,11 +107,11 @@ def tile_dynamiclayer_w_kernel(
             w_tiles[i] = w
             if i == n_chunks - 1:
                 tail_src = Wf_words[6:8].rearrange("g p n t -> p g (n t)")
-                for j in range(4):
-                    wl = lpool.tile([P, 2, NT], U32, tag="wl", name="wl_%d" % j, align_bytes=64)
+                for c0, width in BLOCKS:
+                    wl = lpool.tile([P, 2, width], U32, name="wl_%d" % c0, align_bytes=64)
                     nc.sync.dma_start(
                         out=wl[:].bitcast(I32),
-                        in_=tail_src[:, :, 4 * NT * j : 4 * NT * (j + 1)].bitcast(I32),
+                        in_=tail_src[:, :, 4 * c0 : 4 * (c0 + width)].bitcast(I32),
                     )
                     last_tiles.append(wl)
 
@@ -243,26 +245,36 @@ def tile_dynamiclayer_w_kernel(
 
         oacc = {}
 
-        def out_pass(g, j, rhs):
+        def out_pass(g, b, rhs):
+            c0, width = BLOCKS[b]
             if g == 0:
-                oacc[j] = bank(j, [P, NT], F32, "oacc_%d" % j)
+                oacc[b] = bank(BLOCK_BANK[b], [P, width], F32, "oacc_%d" % b)
             nc.tensor.matmul_mx(
-                out=oacc[j][:],
+                out=oacc[b][:],
                 lhsT=hc[:, P * g : P * (g + 1)].bitcast(FP8X4),
                 lhsT_scale=hsc[:, P * g : P * (g + 1)],
                 rhs=rhs.bitcast(FP8X4),
-                rhs_scale=plf[4 * (g % 4) : P, g // 4, NT * j : NT * (j + 1)],
+                rhs_scale=plf[4 * (g % 4) : P, g // 4, c0 : c0 + width],
                 start=(g == 0),
                 stop=(g == 7),
             )
+
+        def out_passes(g, blocks):
+            for b in blocks:
+                c0, width = BLOCKS[b]
+                out_pass(g, b, w_tiles[12 + g][:, c0 : c0 + width])
 
         for i in range(n_chunks):
             kind, g = chunks[i]
             if i < 3:
                 bias_round(i)
             if kind == "f":
-                for j in range(4):
-                    out_pass(g, j, w_tiles[i][:, NT * j : NT * (j + 1)])
+                out_passes(g, (0, 1, 2, 3))
+                if g == 2:
+                    out_passes(0, (4, 5))
+                    out_passes(1, (4, 5))
+                if g >= 2:
+                    out_passes(g, (4, 5))
             else:
                 first_layer_passes(i)
             if i + W_BUFS < n_chunks:
@@ -277,9 +289,10 @@ def tile_dynamiclayer_w_kernel(
                 requantise(1)
 
         osb = keep.tile([P, D_OUT], F32, name="osb")
-        for j in range(4):
-            out_pass(6, j, last_tiles[j][:, 0, :])
-            out_pass(7, j, last_tiles[j][:, 1, :])
-            cols = slice(NT * j, NT * (j + 1))
-            nc.vector.tensor_tensor(out=osb[:, cols], in0=oacc[j][:], in1=bfb[:, cols], op=ALU.add)
+        for b in range(len(BLOCKS)):
+            c0, width = BLOCKS[b]
+            out_pass(6, b, last_tiles[b][:, 0, :])
+            out_pass(7, b, last_tiles[b][:, 1, :])
+            cols = slice(c0, c0 + width)
+            nc.vector.tensor_tensor(out=osb[:, cols], in0=oacc[b][:], in1=bfb[:, cols], op=ALU.add)
             nc.sync.dma_start(out=out[:, cols], in_=osb[:, cols])

@@ -19,7 +19,7 @@ U2 = 2048
 D_OUT = 2048
 NT = 512
 THRESHOLD = 1.0
-W_BUFS = 14
+W_BUFS = 12
 BLOCKS = ((0, 512), (512, 512), (1024, 512), (1536, 256), (1792, 128), (1920, 128))
 BLOCK_BANK = (0, 1, 2, 3, 5, 6)
 
@@ -86,7 +86,7 @@ def tile_dynamiclayer_w_kernel(
             chunks.append(("a2", kg))
         for kg in range(4):
             chunks.append(("b1", kg))
-        for g in range(6):
+        for g in range(4):
             chunks.append(("f", g))
         n_chunks = len(chunks)
         w_tiles = {}
@@ -106,9 +106,9 @@ def tile_dynamiclayer_w_kernel(
             nc.sync.dma_start(out=w[:].bitcast(I32), in_=src.bitcast(I32))
             w_tiles[i] = w
             if i == n_chunks - 1:
-                tail_src = Wf_words[6:8].rearrange("g p n t -> p g (n t)")
+                tail_src = Wf_words[4:8].rearrange("g p n t -> p g (n t)")
                 for c0, width in BLOCKS:
-                    wl = lpool.tile([P, 2, width], U32, name="wl_%d" % c0, align_bytes=64)
+                    wl = lpool.tile([P, 4, width], U32, name="wl_%d" % c0, align_bytes=64)
                     nc.sync.dma_start(
                         out=wl[:].bitcast(I32),
                         in_=tail_src[:, :, 4 * c0 : 4 * (c0 + width)].bitcast(I32),
@@ -291,8 +291,8 @@ def tile_dynamiclayer_w_kernel(
         osb = keep.tile([P, D_OUT], F32, name="osb")
         for b in range(len(BLOCKS)):
             c0, width = BLOCKS[b]
-            out_pass(6, b, last_tiles[b][:, 0, :])
-            out_pass(7, b, last_tiles[b][:, 1, :])
+            for g in range(4, 8):
+                out_pass(g, b, last_tiles[b][:, g - 4, :])
             cols = slice(c0, c0 + width)
             nc.vector.tensor_tensor(out=osb[:, cols], in0=oacc[b][:], in1=bfb[:, cols], op=ALU.add)
             nc.sync.dma_start(out=out[:, cols], in_=osb[:, cols])

from contextlib import ExitStack

import concourse.mybir as mybir
from concourse.masks import make_identity

FP8X4 = mybir.dt.float8_e4m3fn_x4
F32 = mybir.dt.float32
BF16 = mybir.dt.bfloat16
I32 = mybir.dt.int32
U32 = mybir.dt.uint32
U8 = mybir.dt.uint8
ALU = mybir.AluOpType
ACT = mybir.ActivationFunctionType

P = 128
D_IN = 2048
U1 = 4096
U2 = 2048
D_OUT = 2048
NT = 512
THRESHOLD = 1.0
W_BUFS = 12
BLOCKS = ((0, 512), (512, 512), (1024, 512), (1536, 256), (1792, 128), (1920, 128))
BLOCK_BANK = (0, 1, 2, 3, 5, 6)

FLOPS = 2 * P * (D_IN * U1 + D_IN * U2 + U1 * D_OUT)


def tile_dynamiclayer_w_kernel(
    tc, x, W1_words, W1_scales, b1, W2_words, W2_scales, b2, Wf_words, Wf_scales, bf, out
):
    nc = tc.nc
    with ExitStack() as ctx:
        keep = ctx.enter_context(tc.tile_pool(name="keep", bufs=1))
        wpool = ctx.enter_context(tc.tile_pool(name="wpool", bufs=W_BUFS))
        lpool = ctx.enter_context(tc.tile_pool(name="lpool", bufs=1))
        psum = ctx.enter_context(tc.psum_pool(name="psum", bufs=1))
        ctx.enter_context(tc.manual_schedule())

        def bank(i, shape, dtype, name):
            return psum.tile(shape, dtype, tag="bank%d" % i, name=name)

        warm = keep.tile([P, 1], F32, name="warm")
        warm2 = keep.tile([P, 1], F32, name="warm2")
        pl1 = keep.tile([P, U1], U8, name="pl1", align_bytes=64)
        pl2 = keep.tile([P, U2], U8, name="pl2", align_bytes=64)
        plf = keep.tile([P, 2, D_OUT], U8, name="plf", align_bytes=64)
        sel = keep.tile([P, P], F32, name="sel")
        nc.vector.memset(warm[:], 0.0)
        nc.vector.memset(pl1[:].bitcast(I32), 0)
        nc.vector.memset(pl2[:].bitcast(I32), 0)
        nc.vector.memset(plf[:].bitcast(I32), 0)
        nc.vector.memset(sel[:], 0.0)
        nc.vector.memset(sel[:, 2:3], 1.0)
        nc.scalar.activation(out=warm2[:], in_=warm[:], func=ACT.Abs)

        ident_f = keep.tile([P, P], F32, name="ident_f")
        ident_b = keep.tile([P, P], BF16, name="ident_b")
        brow = keep.tile([P, U1 + D_OUT], BF16, name="brow")
        make_identity(nc, ident_f[:])
        nc.gpsimd.memset(brow[:].bitcast(F32), 0.0)
        make_identity(nc, ident_b[:])

        x_sb = keep.tile([P, D_IN], BF16, name="x_sb")
        nc.sync.dma_start(out=x_sb[:], in_=x)
        for q in (0, 2, 1, 3):
            nc.sync.dma_start(
                out=pl1[32 * q : 32 * q + 16, :].bitcast(I32),
                in_=W1_scales[:, 4 * q : 4 * q + 4, :].bitcast(I32),
            )
        for q in (0, 2, 1, 3):
            nc.sync.dma_start(
                out=pl2[32 * q : 32 * q + 16, :].bitcast(I32),
                in_=W2_scales[:, 4 * q : 4 * q + 4, :].bitcast(I32),
            )
        for a in range(2):
            for q in (0, 2, 1, 3):
                nc.sync.dma_start(
                    out=plf[32 * q : 32 * q + 16, a, :].bitcast(I32),
                    in_=Wf_scales[4 * a : 4 * a + 4, 4 * q : 4 * q + 4, :].bitcast(I32),
                )

        chunks = []
        for kg in range(4):
            chunks.append(("a1", kg))
            chunks.append(("a2", kg))
        for kg in range(4):
            chunks.append(("b1", kg))
        for g in range(4):
            chunks.append(("f", g))
        n_chunks = len(chunks)
        w_tiles = {}
        last_tiles = []

        def load_chunk(i):
            kind, g = chunks[i]
            w = wpool.tile([P, 4 * NT], U32, tag="w", name="w_%s_%d" % (kind, g), align_bytes=64)
            if kind == "a1":
                src = W1_words[g].rearrange("p n t -> p (n t)")[:, 0 : 4 * U2]
            elif kind == "b1":
                src = W1_words[g].rearrange("p n t -> p (n t)")[:, 4 * U2 : 4 * U1]
            elif kind == "a2":
                src = W2_words[g].rearrange("p n t -> p (n t)")
            else:
                src = Wf_words[g].rearrange("p n t -> p (n t)")
            nc.sync.dma_start(out=w[:].bitcast(I32), in_=src.bitcast(I32))
            w_tiles[i] = w
            if i == n_chunks - 1:
                tail_src = Wf_words[4:8].rearrange("g p n t -> p g (n t)")
                for c0, width in BLOCKS:
                    wl = lpool.tile([P, 4, width], U32, name="wl_%d" % c0, align_bytes=64)
                    nc.sync.dma_start(
                        out=wl[:].bitcast(I32),
                        in_=tail_src[:, :, 4 * c0 : 4 * (c0 + width)].bitcast(I32),
                    )
                    last_tiles.append(wl)

        for i in range(W_BUFS):
            load_chunk(i)

        xw = keep.tile([P, 4, 2, P], F32, name="xw")
        nc.vector.tensor_copy(
            out=xw[:], in_=x_sb[:].bitcast(F32).rearrange("b (g p u) -> b g u p", g=4, u=2)
        )
        junk = keep.tile([P, D_IN], BF16, name="junk")
        ssum = keep.tile([P, 1], F32, name="ssum")
        nc.scalar.activation(out=junk[:], in_=x_sb[:], func=ACT.Abs, accum_out=ssum[:])
        nc.scalar.dma_start(out=brow[0:1, 0:U1], in_=b1.rearrange("(o n) -> o n", o=1))
        nc.scalar.dma_start(out=brow[1:2, 0:U2], in_=b2.rearrange("(o n) -> o n", o=1))
        nc.scalar.dma_start(out=brow[2:3, U1 : U1 + D_OUT], in_=bf.rearrange("(o n) -> o n", o=1))
        nc.vector.tensor_single_scalar(
            out=sel[:, 0:1], in_=ssum[:], scalar=THRESHOLD * D_IN, op=ALU.is_gt
        )
        nc.vector.tensor_single_scalar(
            out=sel[:, 1:2], in_=ssum[:], scalar=THRESHOLD * D_IN, op=ALU.is_le
        )
        routes = []
        for a in range(2):
            ia = keep.tile([P, P], F32, name="route_%d" % a)
            nc.vector.tensor_scalar(
                out=ia[:], in0=ident_f[:], scalar1=sel[:, a : a + 1], scalar2=None, op0=ALU.mult
            )
            routes.append(ia)

        selT_ps = bank(4, [P, P], F32, "selT_ps")
        nc.tensor.transpose(selT_ps[:], sel[:], ident_f[:])
        selT = keep.tile([P, P], BF16, name="selT")
        xt = {}
        for a in range(2):
            for gp in range(2):
                t_ps = bank(2 * a + gp, [P, 4, P], F32, "xt_%d_%d" % (a, gp))
                for gi in range(2):
                    for u in range(2):
                        nc.tensor.transpose(
                            t_ps[:, 2 * gi + u, :], xw[:, 2 * gp + gi, u, :], routes[a][:]
                        )
                xt[(a, gp)] = t_ps
        nc.vector.tensor_copy(out=selT[:], in_=selT_ps[:])
        gx = []
        xc = []
        xs = []
        for a in range(2):
            gx.append(keep.tile([P, D_IN], BF16, name="gx_%d" % a, align_bytes=64))
            xc.append(keep.tile([P, D_IN // 4], U32, name="xc_%d" % a, align_bytes=64))
            xs.append(keep.tile([P, D_IN // 4], U8, name="xs_%d" % a, align_bytes=64))
        for a in range(2):
            view = gx[a][:].bitcast(F32).rearrange("p (g r u) -> p g r u", g=4, u=2)
            nc.vector.tensor_copy(
                out=view[:, 0:2, :, :], in_=xt[(a, 0)][:].rearrange("p (g u) r -> p g r u", u=2)
            )
            nc.scalar.copy(
                out=view[:, 2:4, :, :], in_=xt[(a, 1)][:].rearrange("p (g u) r -> p g r u", u=2)
            )
        for a in range(2):
            nc.vector.quantize_mx(out=xc[a][:].bitcast(FP8X4), scales=xs[a][:], in_=gx[a][:])

        bsel = keep.tile([P, 8, 4, P], BF16, name="bsel")
        bfb = keep.tile([P, D_OUT], BF16, name="bfb")

        def bias_round(rnd):
            for c in range(4 * rnd, 4 * rnd + 4):
                pb = bank(4 + c % 4, [P, NT], F32, "pb_%d" % c)
                nc.tensor.matmul(
                    pb[:], lhsT=selT[:], rhs=brow[:, NT * c : NT * (c + 1)], start=True, stop=True
                )
                if c < 8:
                    nc.scalar.copy(
                        out=bsel[:, c, :, :], in_=pb[:].rearrange("b (p t) -> b t p", t=4)
                    )
                else:
                    nc.scalar.copy(out=bfb[:, NT * (c - 8) : NT * (c - 7)], in_=pb[:])

        hs = keep.tile([P, 8, 4, P], BF16, name="hs")
        hg = keep.tile([P, 8, P, 4], BF16, name="hg", align_bytes=64)
        hc = keep.tile([P, 8 * P], U32, name="hc", align_bytes=64)
        hsc = keep.tile([P, 8 * P], U8, name="hsc", align_bytes=64)
        acc = {}

        def first_layer_passes(i):
            kind, kg = chunks[i]
            a = 1 if kind == "a2" else 0
            base = 4 if kind == "b1" else 0
            plane = pl2 if kind == "a2" else pl1
            for j in range(4):
                if (kind == "a1" or kind == "b1") and kg == 0:
                    acc[base + j] = bank(base + j, [P, NT], F32, "acc_%d" % (base + j))
                col = NT * (base + j)
                nc.tensor.matmul_mx(
                    out=acc[base + j][:],
                    lhsT=xc[a][:, P * kg : P * (kg + 1)].bitcast(FP8X4),
                    lhsT_scale=xs[a][:, P * kg : P * (kg + 1)],
                    rhs=w_tiles[i][:, NT * j : NT * (j + 1)].bitcast(FP8X4),
                    rhs_scale=plane[4 * kg : P, col : col + NT],
                    start=((kind == "a1" or kind == "b1") and kg == 0),
                    stop=((kind == "a2" or kind == "b1") and kg == 3),
                )

        def evacuate(half):
            for g in range(4 * half, 4 * half + 4):
                nc.vector.tensor_tensor(
                    out=hs[:, g, :, :],
                    in0=acc[g][:].rearrange("b (p t) -> b t p", t=4),
                    in1=bsel[:, g, :, :],
                    op=ALU.add,
                )

        def requantise(half):
            hts = []
            for g in range(4 * half, 4 * half + 4):
                ht = bank(g, [P, 4, P], BF16, "ht_%d" % g)
                for t in range(4):
                    nc.tensor.transpose(ht[:, t, :], hs[:, g, t, :], ident_b[:])
                hts.append(ht)
            for g in range(4 * half, 4 * half + 4):
                src = hts[g - 4 * half][:].rearrange("p t r -> p r t")
                if g % 2 == 0:
                    nc.scalar.activation(out=hg[:, g, :, :], in_=src, func=ACT.Relu)
                else:
                    nc.vector.tensor_scalar_max(out=hg[:, g, :, :], in0=src, scalar1=0.0)
            nc.vector.quantize_mx(
                out=hc[:, 4 * P * half : 4 * P * (half + 1)].bitcast(FP8X4),
                scales=hsc[:, 4 * P * half : 4 * P * (half + 1)],
                in_=hg[:, 4 * half : 4 * half + 4, :, :].rearrange("p g r t -> p (g r t)"),
            )

        oacc = {}

        def out_pass(g, b, rhs):
            c0, width = BLOCKS[b]
            if g == 0:
                oacc[b] = bank(BLOCK_BANK[b], [P, width], F32, "oacc_%d" % b)
            nc.tensor.matmul_mx(
                out=oacc[b][:],
                lhsT=hc[:, P * g : P * (g + 1)].bitcast(FP8X4),
                lhsT_scale=hsc[:, P * g : P * (g + 1)],
                rhs=rhs.bitcast(FP8X4),
                rhs_scale=plf[4 * (g % 4) : P, g // 4, c0 : c0 + width],
                start=(g == 0),
                stop=(g == 7),
            )

        def out_passes(g, blocks):
            for b in blocks:
                c0, width = BLOCKS[b]
                out_pass(g, b, w_tiles[12 + g][:, c0 : c0 + width])

        for i in range(n_chunks):
            kind, g = chunks[i]
            if i < 3:
                bias_round(i)
            if kind == "f":
                out_passes(g, (0, 1, 2, 3))
                if g == 2:
                    out_passes(0, (4, 5))
                    out_passes(1, (4, 5))
                if g >= 2:
                    out_passes(g, (4, 5))
            else:
                first_layer_passes(i)
            if i + W_BUFS < n_chunks:
                load_chunk(i + W_BUFS)
            if i == 7:
                evacuate(0)
            if i == 8:
                requantise(0)
            if i == 11:
                evacuate(1)
            if i == 12:
                requantise(1)

        osb = keep.tile([P, D_OUT], F32, name="osb")
        for b in range(len(BLOCKS)):
            c0, width = BLOCKS[b]
            for g in range(4, 8):
                out_pass(g, b, last_tiles[b][:, g - 4, :])
            cols = slice(c0, c0 + width)
            nc.vector.tensor_tensor(out=osb[:, cols], in0=oacc[b][:], in1=bfb[:, cols], op=ALU.add)
            nc.sync.dma_start(out=out[:, cols], in_=osb[:, cols])
